import numpy as np
import ml_dtypes


def mxq(x, axis, fmt="e4m3"):
    dtype, down = {"e4m3": (ml_dtypes.float8_e4m3fn, 7), "e5m2": (ml_dtypes.float8_e5m2, 14)}[fmt]
    v = np.moveaxis(np.asarray(x, np.float32).astype(ml_dtypes.bfloat16).astype(np.float64), axis, -1)
    blocks = v.reshape(v.shape[:-1] + (-1, 32))
    amax = np.abs(blocks).max(-1, keepdims=True)
    byte = np.maximum(np.where(amax > 0, np.frexp(amax)[1] - 1 + 127, 0) - down, 1)
    scale = np.exp2(byte - 127.0)
    codes = (blocks / scale).astype(np.float32).astype(dtype).astype(np.float64)
    return np.moveaxis((codes * scale).reshape(v.shape), -1, axis)


WIDE = False


def mx_kscale(k):
    if not WIDE:
        return np.ones(k)
    levels = np.array([10, -10, 5, -5, 0])
    a = np.random.permutation(np.resize(levels, k // 512 * 4)).reshape(k // 512, 4)
    idx = np.arange(k)
    return np.exp2(a[idx // 512, idx % 128 // 32])


BF16 = ml_dtypes.bfloat16


def bf(x):
    return np.asarray(x, np.float32).astype(BF16)


def f64(x):
    return np.asarray(x).astype(np.float64)


B, G, C, F, NC = 8, 16, 512, 128, 4096
HW = G * G
KS = 3
P_GEM = 3.0
EPS_GEM = 1e-6
EPS_NORM = 1e-12


def l2n(v, axis):
    n = np.sqrt(np.sum(v * v, axis=axis, keepdims=True))
    return v / np.maximum(n, EPS_NORM)


def erf(v):
    a = np.clip(v, -7.0, 7.0)
    a2 = 2.0 * a * a
    term = a.copy()
    tot = a.copy()
    for n in range(1, 140):
        term = term * a2 / (2 * n + 1)
        tot = tot + term
    return 2.0 / np.sqrt(np.pi) * np.exp(-a * a) * tot


def gelu_erf(v):
    return 0.5 * v * (1.0 + erf(v / np.sqrt(2.0)))


def setup_inputs():
    s = mx_kscale(C)
    t = s / s.min()
    g = 2.0 ** np.round(0.5 * np.log2(np.mean(t * t)))
    return {"patch_tokens": bf(np.random.standard_normal((B, HW, C)) * 2.0 / G * t),
            "fc1_w": bf(np.random.standard_normal((C, F)) * (g / t)[:, None]),
            "fc1_b": bf(np.random.standard_normal(F) * 0.3)}


def reference(patch_tokens, fc1_w, fc1_b):
    x = f64(patch_tokens)
    padded = np.pad(x.reshape(B, G, G, C), ((0, 0), (KS - 1, 0), (KS // 2, KS // 2), (0, 0)))
    acc = np.zeros_like(x)
    for ki in range(KS):
        for kj in range(KS):
            y = padded[:, ki:ki + G, kj:kj + G, :].reshape(B, HW, C)
            acc = acc + np.maximum(l2n(x * y, 1), EPS_GEM) ** P_GEM
    pooled = (acc / (KS * KS)) ** (1.0 / P_GEM)
    tokens = l2n(pooled + x, 2)
    return gelu_erf((mxq(tokens, 2, "e4m3") @ mxq(f64(fc1_w), 0, "e4m3")) + f64(fc1_b))

@@ -1,0 +1,348 @@
+from contextlib import ExitStack
+
+import concourse.mybir as mybir
+from concourse.masks import make_identity
+
+F32 = mybir.dt.float32
+BF16 = mybir.dt.bfloat16
+U32 = mybir.dt.uint32
+U8 = mybir.dt.uint8
+FP8X4 = mybir.dt.float8_e4m3fn_x4
+ALU = mybir.AluOpType
+ACT = mybir.ActivationFunctionType
+
+P = 128
+B = 8
+GRID = 16
+T = GRID * GRID
+H = T // P
+C = 512
+CH = C // P
+F = 128
+PACK = 4
+
+FLOPS = 2 * B * T * C * F
+
+OFFSETS = [(0, 0), (0, -1), (-1, -1), (-1, 0), (-1, 1), (-2, -1), (-2, 0), (-2, 1)]
+K = len(OFFSETS)
+K_LEFT = OFFSETS.index((0, -1))
+TERMS = [(k, 0) for k in range(K)] + [(K_LEFT, 1)]
+
+PADDED = GRID + 2
+CUBE_COLS = T + 4
+
+EPS_GEM_CUBED = 1e-18
+EPS_NORM_SQUARED = 1e-24
+
+ROUND = 2
+Z_PER_QUARTER = 3
+Z_ON_VECTOR = 6
+
+
+def tile_tokenmudule_pa_s_kernel(tc, patch_tokens, fc1_w, fc1_b, out):
+    nc = tc.nc
+    assert CH == ROUND + 2
+
+    with ExitStack() as ctx:
+        ctx.enter_context(tc.manual_schedule())
+
+        def sbuf(name, bufs):
+            return ctx.enter_context(tc.tile_pool(name=name, bufs=bufs))
+
+        def psum(name, bufs):
+            return ctx.enter_context(tc.psum_pool(name=name, bufs=bufs))
+
+        keep = sbuf("keep", 1)
+        sq_pool = sbuf("sq", 2)
+        cube_nat_pool = sbuf("cube_nat", 3)
+        z_pool = sbuf("z", 4)
+        coef_pool = sbuf("coef", 2)
+        sum_pool = sbuf("sum", 4)
+        tail_pool = sbuf("tail", 2)
+        xT_psum = psum("xT_psum", 1)
+        pT_psum = psum("pT_psum", 2)
+        acc_psum = psum("acc_psum", 4)
+        proj_psum = psum("proj_psum", 1)
+
+        x_nat = keep.tile([P, B, H, C], BF16)
+        for b in range(B):
+            nc.sync.dma_start(
+                out=x_nat[:, b], in_=patch_tokens[b].rearrange("(h p) c -> p h c", p=P)
+            )
+        w_raw = keep.tile([P, PACK, F], BF16)
+        nc.scalar.dma_start(out=w_raw[:], in_=fc1_w.rearrange("(t p) f -> p t f", p=P))
+        bias = keep.tile([P, F], BF16)
+        nc.scalar.dma_start(out=bias[:], in_=fc1_b.partition_broadcast(P))
+
+        ident_bf = keep.tile([P, P], BF16)
+        make_identity(nc, ident_bf[:])
+        ident_f = keep.tile([P, P], F32)
+        make_identity(nc, ident_f[:])
+
+        x_pad = [keep.tile([P, CH, GRID, PADDED], BF16, name="x_pad%d" % i) for i in range(2)]
+        p_pad = [keep.tile([P, GRID, PADDED], F32, name="p_pad%d" % i) for i in range(2)]
+        cubes = [keep.tile([P, K, CUBE_COLS], F32, name="cubes%d" % i) for i in range(3)]
+        for zeroed in x_pad + p_pad + cubes:
+            nc.vector.memset(zeroed[:], 0.0)
+
+        w_grouped = keep.tile([P, F, PACK], BF16, align_bytes=64)
+        w_codes = keep.tile([P, F], U32, align_bytes=64)
+        w_scales = keep.tile([P, F], U8, align_bytes=64)
+        nc.vector.tensor_copy(out=w_grouped[:], in_=w_raw[:].rearrange("p t f -> p f t"))
+        nc.vector.quantize_mx(
+            out=w_codes[:].bitcast(FP8X4),
+            scales=w_scales[:],
+            in_=w_grouped[:].rearrange("p f t -> p (f t)"),
+        )
+
+        pre_act = keep.tile([P, B, H, F], F32)
+        result = keep.tile([P, B, H, F], F32)
+
+        xT = {}
+        p_nat = {}
+        norm_sq = {}
+        inv_norm = {}
+        coef = {}
+        pT = {}
+        acc = {}
+        pooled = {}
+
+        def grid(ap):
+            return ap.rearrange("p (i j) -> p i j", j=GRID)
+
+        def grids(ap):
+            return ap.rearrange("p c (i j) -> p c i j", j=GRID)
+
+        def transpose_x(b):
+            xT[b] = xT_psum.tile([P, CH, T], BF16, name="xT")
+            for h in range(H):
+                for ch in range(CH):
+                    nc.tensor.transpose(
+                        xT[b][:, ch, h * P : (h + 1) * P],
+                        x_nat[:, b, h, ch * P : (ch + 1) * P],
+                        ident_bf[:],
+                    )
+            nc.scalar.copy(out=x_pad[b % 2][:, :, :, 1 : 1 + GRID], in_=grids(xT[b][:]))
+
+        def cube_x(b):
+            squared = sq_pool.tile([P, H, C], F32, name="squared")
+            nc.scalar.activation(out=squared[:], in_=x_nat[:, b], func=ACT.Square)
+            p_nat[b] = cube_nat_pool.tile([P, H, C], F32, name="p_nat")
+            nc.gpsimd.tensor_tensor(out=p_nat[b][:], in0=squared[:], in1=x_nat[:, b], op=ALU.mult)
+
+        def square_products(b, k):
+            if k == 0:
+                norm_sq[b] = coef_pool.tile([P, K, CH], F32, name="norm_sq")
+            di, dj = OFFSETS[k]
+            top = -di
+            z = z_pool.tile([P, CH, T], F32, name="z")
+            neighbour = x_pad[b % 2][:, :, 0 : GRID - top, 1 + dj : 1 + dj + GRID]
+            if k < Z_ON_VECTOR:
+                nc.vector.tensor_tensor(
+                    out=grids(z[:, :, top * GRID :]),
+                    in0=grids(xT[b][:, :, top * GRID :]),
+                    in1=neighbour,
+                    op=ALU.mult,
+                )
+            else:
+                nc.gpsimd.tensor_tensor(
+                    out=grids(z[:, :, top * GRID :]),
+                    in0=x_pad[b % 2][:, :, top:GRID, 1 : 1 + GRID],
+                    in1=neighbour,
+                    op=ALU.mult,
+                )
+            for ch in range(CH):
+                nc.scalar.activation(
+                    out=z[:, ch, top * GRID :],
+                    in_=z[:, ch, top * GRID :],
+                    func=ACT.Square,
+                    accum_out=norm_sq[b][:, k, ch : ch + 1],
+                )
+
+        def inverse_root(pool, squares, shape, name):
+            floored = pool.tile(shape, F32, name=name + "_floored")
+            nc.vector.tensor_scalar_max(floored[:], squares, EPS_NORM_SQUARED)
+            root = pool.tile(shape, F32, name=name + "_root")
+            nc.scalar.activation(out=root[:], in_=floored[:], func=ACT.Sqrt)
+            inverse = pool.tile(shape, F32, name=name + "_inverse")
+            nc.vector.reciprocal(inverse[:], root[:])
+            return root, inverse
+
+        def coefficients(b):
+            root, inv_norm[b] = inverse_root(coef_pool, norm_sq[b][:], [P, K, CH], "n")
+            ratio = coef_pool.tile([P, K, CH], F32, name="ratio")
+            nc.vector.tensor_tensor(
+                out=ratio[:],
+                in0=inv_norm[b][:],
+                in1=root[:, 0:1, :].to_broadcast([P, K, CH]),
+                op=ALU.mult,
+            )
+            inv_sq = coef_pool.tile([P, K, CH], F32, name="inv_sq")
+            nc.vector.tensor_tensor(
+                out=inv_sq[:], in0=inv_norm[b][:], in1=inv_norm[b][:], op=ALU.mult
+            )
+            coef[b] = coef_pool.tile([P, K, CH], F32, name="coef")
+            nc.vector.tensor_tensor(out=coef[b][:], in0=ratio[:], in1=inv_sq[:], op=ALU.mult)
+
+        def transpose_p(b, ch):
+            pT[b, ch] = pT_psum.tile([P, T], F32, name="pT")
+            for h in range(H):
+                nc.tensor.transpose(
+                    pT[b, ch][:, h * P : (h + 1) * P],
+                    p_nat[b][:, h, ch * P : (ch + 1) * P],
+                    ident_f[:],
+                )
+            nc.scalar.activation(
+                out=p_pad[(b * CH + ch) % 2][:, :, 1 : 1 + GRID],
+                in_=grid(pT[b, ch][:]),
+                func=ACT.Copy,
+                scale=inv_norm[b][:, 0, ch : ch + 1],
+            )
+
+        def window_terms(b, ch):
+            terms = cubes[(b * CH + ch) % 3]
+            for k in range(K):
+                di, dj = OFFSETS[k]
+                top = -di
+                nc.vector.scalar_tensor_tensor(
+                    out=grid(terms[:, k, top * GRID : T]),
+                    in0=grid(pT[b, ch][:, top * GRID :]),
+                    scalar=coef[b][:, k, ch : ch + 1],
+                    in1=p_pad[(b * CH + ch) % 2][:, 0 : GRID - top, 1 + dj : 1 + dj + GRID],
+                    op0=ALU.mult,
+                    op1=ALU.mult,
+                )
+            nc.gpsimd.tensor_scalar(
+                out=terms[:],
+                in0=terms[:],
+                scalar1=EPS_GEM_CUBED,
+                scalar2=0.0,
+                op0=ALU.max,
+                op1=ALU.add,
+            )
+
+        def window_sum(b, ch):
+            terms = cubes[(b * CH + ch) % 3]
+            if ch == 0:
+                for h in range(H):
+                    acc[b, h] = acc_psum.tile([P, C], F32, name="acc")
+            for i, (k, ahead) in enumerate(TERMS):
+                for h in range(H):
+                    nc.tensor.matmul(
+                        acc[b, h][:, ch * P : (ch + 1) * P],
+                        lhsT=terms[:, k, ahead + h * P : ahead + (h + 1) * P],
+                        rhs=ident_f[:],
+                        is_transpose=True,
+                        start=(i == 0),
+                        stop=(i == len(TERMS) - 1),
+                    )
+
+        def save_sum(b):
+            pooled[b] = sum_pool.tile([P, H, C], F32, name="pooled")
+            for h in range(H):
+                nc.scalar.copy(out=pooled[b][:, h, :], in_=acc[b, h][:])
+
+        def logarithm(b):
+            nc.scalar.activation(
+                out=pooled[b][:], in_=pooled[b][:], func=ACT.Ln, scale=1.0 / len(TERMS)
+            )
+
+        def cube_root(b):
+            nc.scalar.activation(out=pooled[b][:], in_=pooled[b][:], func=ACT.Exp, scale=1.0 / 3.0)
+
+        def project(b):
+            r = pooled[b]
+            nc.gpsimd.tensor_tensor(out=r[:], in0=r[:], in1=x_nat[:, b], op=ALU.add)
+            unused = tail_pool.tile([P, H, C], BF16, name="unused")
+            r_sq = tail_pool.tile([P, H], F32, name="r_sq")
+            for h in range(H):
+                nc.scalar.activation(
+                    out=unused[:, h, :],
+                    in_=r[:, h, :],
+                    func=ACT.Square,
+                    accum_out=r_sq[:, h : h + 1],
+                )
+            inv_r = inverse_root(tail_pool, r_sq[:], [P, H], "r")[1]
+            tokens = tail_pool.tile([P, H, C], BF16, name="tokens")
+            for h in range(H):
+                nc.scalar.activation(
+                    out=tokens[:, h, :], in_=r[:, h, :], func=ACT.Copy, scale=inv_r[:, h : h + 1]
+                )
+            tokT = proj_psum.tile([P, H, PACK, P], BF16, name="proj")
+            for h in range(H):
+                for t in range(PACK):
+                    nc.tensor.transpose(
+                        tokT[:, h, t, :], tokens[:, h, t * P : (t + 1) * P], ident_bf[:]
+                    )
+            grouped = tail_pool.tile([P, H, P, PACK], BF16, name="grouped", align_bytes=64)
+            nc.vector.tensor_copy(out=grouped[:], in_=tokT[:].rearrange("p h t r -> p h r t"))
+            codes = tail_pool.tile([P, H * P], U32, name="codes", align_bytes=64)
+            scales = tail_pool.tile([P, H * P], U8, name="scales", align_bytes=64)
+            nc.vector.quantize_mx(
+                out=codes[:].bitcast(FP8X4),
+                scales=scales[:],
+                in_=grouped[:].rearrange("p h r t -> p (h r t)"),
+            )
+            product = proj_psum.tile([P, H, F], F32, name="proj")
+            for h in range(H):
+                nc.tensor.matmul_mx(
+                    out=product[:, h, :],
+                    lhsT=codes[:, h * P : (h + 1) * P].bitcast(FP8X4),
+                    lhsT_scale=scales[:, h * P : (h + 1) * P],
+                    rhs=w_codes[:].bitcast(FP8X4),
+                    rhs_scale=w_scales[:],
+                    start=True,
+                    stop=True,
+                )
+            nc.vector.tensor_tensor(
+                out=pre_act[:, b],
+                in0=product[:],
+                in1=bias[:].unsqueeze(1).to_broadcast([P, H, F]),
+                op=ALU.add,
+            )
+
+        def close_round(first, step):
+            if step == 0:
+                for b in range(first, first + ROUND):
+                    logarithm(b)
+            elif step == 1:
+                for b in range(first, first + ROUND):
+                    cube_root(b)
+            else:
+                project(first + step - 2)
+
+        transpose_x(0)
+        cube_x(0)
+        for k in range(K):
+            square_products(0, k)
+        coefficients(0)
+        transpose_p(0, 0)
+        transpose_x(1)
+        cube_x(1)
+
+        for b in range(B):
+            for ch in range(CH):
+                if b + 1 < B:
+                    for k in range(ch * Z_PER_QUARTER, min(K, (ch + 1) * Z_PER_QUARTER)):
+                        square_products(b + 1, k)
+                window_terms(b, ch)
+                if ch + 1 < CH:
+                    transpose_p(b, ch + 1)
+                elif b + 1 < B:
+                    coefficients(b + 1)
+                    transpose_p(b + 1, 0)
+                    if b + 2 < B:
+                        transpose_x(b + 2)
+                        cube_x(b + 2)
+                window_sum(b, ch)
+                if b >= ROUND and b % ROUND == 0:
+                    close_round(b - ROUND, ch)
+            save_sum(b)
+        for step in range(CH):
+            close_round(B - ROUND, step)
+
+        stored = out.rearrange("b (h p) f -> p b h f", p=P)
+        for first in range(0, B, ROUND):
+            images = slice(first, first + ROUND)
+            nc.scalar.activation(out=result[:, images], in_=pre_act[:, images], func=ACT.Gelu)
+            nc.sync.dma_start(out=stored[:, images], in_=result[:, images])

@@ -29,19 +29,18 @@ K_LEFT = OFFSETS.index((0, -1))
 TERMS = [(k, 0) for k in range(K)] + [(K_LEFT, 1)]
 
 PADDED = GRID + 2
-CUBE_COLS = T + 4
+TERM_COLS = T + 4
 
 EPS_GEM_CUBED = 1e-18
 EPS_NORM_SQUARED = 1e-24
 
+PAIR = 2
 ROUND = 2
-Z_PER_QUARTER = 3
-Z_ON_VECTOR = 6
+CLOSING_STEPS = 7
 
 
 def tile_tokenmudule_pa_s_kernel(tc, patch_tokens, fc1_w, fc1_b, out):
     nc = tc.nc
-    assert CH == ROUND + 2
 
     with ExitStack() as ctx:
         ctx.enter_context(tc.manual_schedule())
@@ -53,16 +52,13 @@ def tile_tokenmudule_pa_s_kernel(tc, patch_tokens, fc1_w, fc1_b, out):
             return ctx.enter_context(tc.psum_pool(name=name, bufs=bufs))
 
         keep = sbuf("keep", 1)
-        sq_pool = sbuf("sq", 2)
-        cube_nat_pool = sbuf("cube_nat", 3)
-        z_pool = sbuf("z", 4)
+        unread_pool = sbuf("unread", 4)
         coef_pool = sbuf("coef", 2)
-        sum_pool = sbuf("sum", 4)
-        tail_pool = sbuf("tail", 2)
-        xT_psum = psum("xT_psum", 1)
-        pT_psum = psum("pT_psum", 2)
-        acc_psum = psum("acc_psum", 4)
-        proj_psum = psum("proj_psum", 1)
+        pooled_pool = sbuf("pooled", 2 * ROUND)
+        tail_pool = sbuf("tail", ROUND)
+        xT_psum = psum("xT_psum", 2)
+        acc_psum = psum("acc_psum", ROUND * H)
+        proj_psum = psum("proj_psum", 2)
 
         x_nat = keep.tile([P, B, H, C], BF16)
         for b in range(B):
@@ -78,11 +74,17 @@ def tile_tokenmudule_pa_s_kernel(tc, patch_tokens, fc1_w, fc1_b, out):
         make_identity(nc, ident_bf[:])
         ident_f = keep.tile([P, P], F32)
         make_identity(nc, ident_f[:])
+        plus_eps = keep.tile([P, 1], F32)
+        nc.vector.memset(plus_eps[:], EPS_GEM_CUBED)
+        minus_eps = keep.tile([P, 1], F32)
+        nc.vector.memset(minus_eps[:], -EPS_GEM_CUBED)
 
-        x_pad = [keep.tile([P, CH, GRID, PADDED], BF16, name="x_pad%d" % i) for i in range(2)]
-        p_pad = [keep.tile([P, GRID, PADDED], F32, name="p_pad%d" % i) for i in range(2)]
-        cubes = [keep.tile([P, K, CUBE_COLS], F32, name="cubes%d" % i) for i in range(3)]
-        for zeroed in x_pad + p_pad + cubes:
+        q_pad = [keep.tile([P, CH, GRID, PADDED], F32, name="q_pad%d" % i) for i in range(2)]
+        p_pad = [keep.tile([P, CH, GRID, PADDED], F32, name="p_pad%d" % i) for i in range(2)]
+        term_tiles = [
+            keep.tile([P, K, PAIR, TERM_COLS], F32, name="terms%d" % i) for i in range(3)
+        ]
+        for zeroed in q_pad + p_pad + term_tiles:
             nc.vector.memset(zeroed[:], 0.0)
 
         w_grouped = keep.tile([P, F, PACK], BF16, align_bytes=64)
@@ -99,21 +101,23 @@ def tile_tokenmudule_pa_s_kernel(tc, patch_tokens, fc1_w, fc1_b, out):
         result = keep.tile([P, B, H, F], F32)
 
         xT = {}
-        p_nat = {}
+        own_sq = {}
         norm_sq = {}
+        norm = {}
         inv_norm = {}
         coef = {}
-        pT = {}
         acc = {}
         pooled = {}
+        closing = {}
+        steps_done = {}
 
         def grid(ap):
             return ap.rearrange("p (i j) -> p i j", j=GRID)
 
-        def grids(ap):
-            return ap.rearrange("p c (i j) -> p c i j", j=GRID)
+        def shifted(padded, top, dj):
+            return padded[:, 0 : GRID - top, 1 + dj : 1 + dj + GRID]
 
-        def transpose_x(b):
+        def prepare(b):
             xT[b] = xT_psum.tile([P, CH, T], BF16, name="xT")
             for h in range(H):
                 for ch in range(CH):
@@ -122,224 +126,240 @@ def tile_tokenmudule_pa_s_kernel(tc, patch_tokens, fc1_w, fc1_b, out):
                         x_nat[:, b, h, ch * P : (ch + 1) * P],
                         ident_bf[:],
                     )
-            nc.scalar.copy(out=x_pad[b % 2][:, :, :, 1 : 1 + GRID], in_=grids(xT[b][:]))
+            q = q_pad[b % 2]
+            nc.scalar.activation(
+                out=q[:, :, :, 1 : 1 + GRID],
+                in_=xT[b][:].rearrange("p c (i j) -> p c i j", j=GRID),
+                func=ACT.Square,
+            )
+            own_sq[b] = coef_pool.tile([P, CH], F32, name="own_sq")
+            for ch in range(CH):
+                unread = unread_pool.tile([P, GRID, PADDED], BF16, name="unread_s")
+                nc.scalar.activation(
+                    out=unread[:],
+                    in_=q[:, ch],
+                    func=ACT.Square,
+                    accum_out=own_sq[b][:, ch : ch + 1],
+                )
 
-        def cube_x(b):
-            squared = sq_pool.tile([P, H, C], F32, name="squared")
-            nc.scalar.activation(out=squared[:], in_=x_nat[:, b], func=ACT.Square)
-            p_nat[b] = cube_nat_pool.tile([P, H, C], F32, name="p_nat")
-            nc.gpsimd.tensor_tensor(out=p_nat[b][:], in0=squared[:], in1=x_nat[:, b], op=ALU.mult)
-
-        def square_products(b, k):
-            if k == 0:
+        def sum_products(b, k):
+            if k == 1:
                 norm_sq[b] = coef_pool.tile([P, K, CH], F32, name="norm_sq")
             di, dj = OFFSETS[k]
             top = -di
-            z = z_pool.tile([P, CH, T], F32, name="z")
-            neighbour = x_pad[b % 2][:, :, 0 : GRID - top, 1 + dj : 1 + dj + GRID]
-            if k < Z_ON_VECTOR:
-                nc.vector.tensor_tensor(
-                    out=grids(z[:, :, top * GRID :]),
-                    in0=grids(xT[b][:, :, top * GRID :]),
-                    in1=neighbour,
-                    op=ALU.mult,
-                )
-            else:
-                nc.gpsimd.tensor_tensor(
-                    out=grids(z[:, :, top * GRID :]),
-                    in0=x_pad[b % 2][:, :, top:GRID, 1 : 1 + GRID],
-                    in1=neighbour,
-                    op=ALU.mult,
-                )
+            q = q_pad[b % 2]
             for ch in range(CH):
-                nc.scalar.activation(
-                    out=z[:, ch, top * GRID :],
-                    in_=z[:, ch, top * GRID :],
-                    func=ACT.Square,
+                unread = unread_pool.tile([P, GRID, GRID], F32, name="unread_v")
+                nc.vector.scalar_tensor_tensor(
+                    out=unread[:, top:GRID, :],
+                    in0=q[:, ch, top:GRID, 1 : 1 + GRID],
+                    scalar=1.0,
+                    in1=shifted(q[:, ch], top, dj),
+                    op0=ALU.mult,
+                    op1=ALU.mult,
                     accum_out=norm_sq[b][:, k, ch : ch + 1],
                 )
 
-        def inverse_root(pool, squares, shape, name):
-            floored = pool.tile(shape, F32, name=name + "_floored")
-            nc.vector.tensor_scalar_max(floored[:], squares, EPS_NORM_SQUARED)
-            root = pool.tile(shape, F32, name=name + "_root")
-            nc.scalar.activation(out=root[:], in_=floored[:], func=ACT.Sqrt)
-            inverse = pool.tile(shape, F32, name=name + "_inverse")
-            nc.vector.reciprocal(inverse[:], root[:])
-            return root, inverse
+        def start_coefficients(b):
+            floored = coef_pool.tile([P, K, CH], F32, name="n_floored")
+            nc.vector.tensor_scalar_max(floored[:, 0, :], own_sq[b][:], EPS_NORM_SQUARED)
+            nc.vector.tensor_scalar_max(floored[:, 1:K, :], norm_sq[b][:, 1:K, :], EPS_NORM_SQUARED)
+            norm[b] = coef_pool.tile([P, K, CH], F32, name="norm")
+            nc.scalar.activation(out=norm[b][:], in_=floored[:], func=ACT.Sqrt)
 
-        def coefficients(b):
-            root, inv_norm[b] = inverse_root(coef_pool, norm_sq[b][:], [P, K, CH], "n")
+        def finish_coefficients(b):
+            inv_norm[b] = coef_pool.tile([P, K, CH], F32, name="inv_norm")
+            nc.vector.reciprocal(inv_norm[b][:], norm[b][:])
             ratio = coef_pool.tile([P, K, CH], F32, name="ratio")
             nc.vector.tensor_tensor(
                 out=ratio[:],
                 in0=inv_norm[b][:],
-                in1=root[:, 0:1, :].to_broadcast([P, K, CH]),
+                in1=norm[b][:, 0:1, :].to_broadcast([P, K, CH]),
                 op=ALU.mult,
             )
-            inv_sq = coef_pool.tile([P, K, CH], F32, name="inv_sq")
-            nc.vector.tensor_tensor(
-                out=inv_sq[:], in0=inv_norm[b][:], in1=inv_norm[b][:], op=ALU.mult
-            )
+            ratio_sq = coef_pool.tile([P, K, CH], F32, name="ratio_sq")
+            nc.vector.tensor_tensor(out=ratio_sq[:], in0=ratio[:], in1=ratio[:], op=ALU.mult)
             coef[b] = coef_pool.tile([P, K, CH], F32, name="coef")
-            nc.vector.tensor_tensor(out=coef[b][:], in0=ratio[:], in1=inv_sq[:], op=ALU.mult)
-
-        def transpose_p(b, ch):
-            pT[b, ch] = pT_psum.tile([P, T], F32, name="pT")
-            for h in range(H):
-                nc.tensor.transpose(
-                    pT[b, ch][:, h * P : (h + 1) * P],
-                    p_nat[b][:, h, ch * P : (ch + 1) * P],
-                    ident_f[:],
-                )
-            nc.scalar.activation(
-                out=p_pad[(b * CH + ch) % 2][:, :, 1 : 1 + GRID],
-                in_=grid(pT[b, ch][:]),
-                func=ACT.Copy,
-                scale=inv_norm[b][:, 0, ch : ch + 1],
+            nc.vector.tensor_tensor(
+                out=coef[b][:], in0=ratio_sq[:], in1=inv_norm[b][:], op=ALU.mult
             )
 
-        def window_terms(b, ch):
-            terms = cubes[(b * CH + ch) % 3]
-            for k in range(K):
-                di, dj = OFFSETS[k]
-                top = -di
+        def scale_cubes(b):
+            for ch in range(CH):
                 nc.vector.scalar_tensor_tensor(
-                    out=grid(terms[:, k, top * GRID : T]),
-                    in0=grid(pT[b, ch][:, top * GRID :]),
-                    scalar=coef[b][:, k, ch : ch + 1],
-                    in1=p_pad[(b * CH + ch) % 2][:, 0 : GRID - top, 1 + dj : 1 + dj + GRID],
+                    out=p_pad[b % 2][:, ch, :, 1 : 1 + GRID],
+                    in0=q_pad[b % 2][:, ch, :, 1 : 1 + GRID],
+                    scalar=inv_norm[b][:, 0, ch : ch + 1],
+                    in1=grid(xT[b][:, ch, :]),
                     op0=ALU.mult,
                     op1=ALU.mult,
                 )
-            nc.gpsimd.tensor_scalar(
-                out=terms[:],
-                in0=terms[:],
-                scalar1=EPS_GEM_CUBED,
-                scalar2=0.0,
-                op0=ALU.max,
-                op1=ALU.add,
-            )
 
-        def window_sum(b, ch):
-            terms = cubes[(b * CH + ch) % 3]
-            if ch == 0:
+        def window_terms(b, pair):
+            terms = term_tiles[(b * (CH // PAIR) + pair) % 3]
+            chunks = slice(pair * PAIR, (pair + 1) * PAIR)
+            p = p_pad[b % 2]
+            for k in range(K):
+                di, dj = OFFSETS[k]
+                top = -di
+                nc.vector.tensor_tensor(
+                    out=terms[:, k, :, top * GRID : T].rearrange("p c (i j) -> p c i j", j=GRID),
+                    in0=p[:, chunks, top:GRID, 1 : 1 + GRID],
+                    in1=p[:, chunks, 0 : GRID - top, 1 + dj : 1 + dj + GRID],
+                    op=ALU.mult,
+                )
+                for c in range(PAIR):
+                    nc.scalar.activation(
+                        out=terms[:, k, c, top * GRID : T],
+                        in_=terms[:, k, c, top * GRID : T],
+                        func=ACT.Relu,
+                        scale=coef[b][:, k, pair * PAIR + c : pair * PAIR + c + 1],
+                        bias=minus_eps[:],
+                    )
+
+        def window_sum(b, pair):
+            terms = term_tiles[(b * (CH // PAIR) + pair) % 3]
+            if pair == 0:
                 for h in range(H):
                     acc[b, h] = acc_psum.tile([P, C], F32, name="acc")
-            for i, (k, ahead) in enumerate(TERMS):
-                for h in range(H):
-                    nc.tensor.matmul(
-                        acc[b, h][:, ch * P : (ch + 1) * P],
-                        lhsT=terms[:, k, ahead + h * P : ahead + (h + 1) * P],
-                        rhs=ident_f[:],
-                        is_transpose=True,
-                        start=(i == 0),
-                        stop=(i == len(TERMS) - 1),
-                    )
+            for c in range(PAIR):
+                ch = pair * PAIR + c
+                for i, (k, ahead) in enumerate(TERMS):
+                    for h in range(H):
+                        nc.tensor.matmul(
+                            acc[b, h][:, ch * P : (ch + 1) * P],
+                            lhsT=terms[:, k, c, ahead + h * P : ahead + (h + 1) * P],
+                            rhs=ident_f[:],
+                            is_transpose=True,
+                            start=(i == 0),
+                            stop=(i == len(TERMS) - 1),
+                        )
 
-        def save_sum(b):
-            pooled[b] = sum_pool.tile([P, H, C], F32, name="pooled")
-            for h in range(H):
-                nc.scalar.copy(out=pooled[b][:, h, :], in_=acc[b, h][:])
-
-        def logarithm(b):
-            nc.scalar.activation(
-                out=pooled[b][:], in_=pooled[b][:], func=ACT.Ln, scale=1.0 / len(TERMS)
-            )
-
-        def cube_root(b):
-            nc.scalar.activation(out=pooled[b][:], in_=pooled[b][:], func=ACT.Exp, scale=1.0 / 3.0)
-
-        def project(b):
-            r = pooled[b]
-            nc.gpsimd.tensor_tensor(out=r[:], in0=r[:], in1=x_nat[:, b], op=ALU.add)
-            unused = tail_pool.tile([P, H, C], BF16, name="unused")
-            r_sq = tail_pool.tile([P, H], F32, name="r_sq")
-            for h in range(H):
-                nc.scalar.activation(
-                    out=unused[:, h, :],
-                    in_=r[:, h, :],
-                    func=ACT.Square,
-                    accum_out=r_sq[:, h : h + 1],
-                )
-            inv_r = inverse_root(tail_pool, r_sq[:], [P, H], "r")[1]
-            tokens = tail_pool.tile([P, H, C], BF16, name="tokens")
-            for h in range(H):
-                nc.scalar.activation(
-                    out=tokens[:, h, :], in_=r[:, h, :], func=ACT.Copy, scale=inv_r[:, h : h + 1]
-                )
-            tokT = proj_psum.tile([P, H, PACK, P], BF16, name="proj")
-            for h in range(H):
-                for t in range(PACK):
-                    nc.tensor.transpose(
-                        tokT[:, h, t, :], tokens[:, h, t * P : (t + 1) * P], ident_bf[:]
-                    )
-            grouped = tail_pool.tile([P, H, P, PACK], BF16, name="grouped", align_bytes=64)
-            nc.vector.tensor_copy(out=grouped[:], in_=tokT[:].rearrange("p h t r -> p h r t"))
-            codes = tail_pool.tile([P, H * P], U32, name="codes", align_bytes=64)
-            scales = tail_pool.tile([P, H * P], U8, name="scales", align_bytes=64)
-            nc.vector.quantize_mx(
-                out=codes[:].bitcast(FP8X4),
-                scales=scales[:],
-                in_=grouped[:].rearrange("p h r t -> p (h r t)"),
-            )
-            product = proj_psum.tile([P, H, F], F32, name="proj")
-            for h in range(H):
-                nc.tensor.matmul_mx(
-                    out=product[:, h, :],
-                    lhsT=codes[:, h * P : (h + 1) * P].bitcast(FP8X4),
-                    lhsT_scale=scales[:, h * P : (h + 1) * P],
-                    rhs=w_codes[:].bitcast(FP8X4),
-                    rhs_scale=w_scales[:],
-                    start=True,
-                    stop=True,
-                )
-            nc.vector.tensor_tensor(
-                out=pre_act[:, b],
-                in0=product[:],
-                in1=bias[:].unsqueeze(1).to_broadcast([P, H, F]),
-                op=ALU.add,
-            )
-
-        def close_round(first, step):
+        def close_round(first):
+            step = steps_done.get(first, 0)
+            steps_done[first] = step + 1
+            images = range(first, first + ROUND)
             if step == 0:
-                for b in range(first, first + ROUND):
-                    logarithm(b)
+                for b in images:
+                    pooled[b] = pooled_pool.tile([P, H, C], F32, name="pooled")
+                    for h in range(H):
+                        nc.scalar.activation(
+                            out=pooled[b][:, h, :],
+                            in_=acc[b, h][:],
+                            func=ACT.Ln,
+                            scale=1.0 / len(TERMS),
+                            bias=plus_eps[:],
+                        )
             elif step == 1:
-                for b in range(first, first + ROUND):
-                    cube_root(b)
+                for b in images:
+                    nc.scalar.activation(
+                        out=pooled[b][:], in_=pooled[b][:], func=ACT.Exp, scale=1.0 / 3.0
+                    )
+            elif step == 2:
+                r_sq = tail_pool.tile([P, ROUND, H], F32, name="r_sq")
+                closing[first, "r_sq"] = r_sq
+                for b in images:
+                    nc.vector.tensor_tensor(
+                        out=pooled[b][:], in0=pooled[b][:], in1=x_nat[:, b], op=ALU.add
+                    )
+                    unread = tail_pool.tile([P, H, C], BF16, name="unread_r")
+                    for h in range(H):
+                        nc.scalar.activation(
+                            out=unread[:, h, :],
+                            in_=pooled[b][:, h, :],
+                            func=ACT.Square,
+                            accum_out=r_sq[:, b - first, h : h + 1],
+                        )
+            elif step == 3:
+                floored = tail_pool.tile([P, ROUND, H], F32, name="r_floored")
+                nc.vector.tensor_scalar_max(floored[:], closing[first, "r_sq"][:], EPS_NORM_SQUARED)
+                r_norm = tail_pool.tile([P, ROUND, H], F32, name="r_norm")
+                closing[first, "r_norm"] = r_norm
+                nc.scalar.activation(out=r_norm[:], in_=floored[:], func=ACT.Sqrt)
+            elif step == 4:
+                inv_r = tail_pool.tile([P, ROUND, H], F32, name="inv_r")
+                nc.vector.reciprocal(inv_r[:], closing[first, "r_norm"][:])
+                for b in images:
+                    tokens = tail_pool.tile([P, H, C], BF16, name="tokens")
+                    closing[b, "tokens"] = tokens
+                    for h in range(H):
+                        nc.scalar.activation(
+                            out=tokens[:, h, :],
+                            in_=pooled[b][:, h, :],
+                            func=ACT.Copy,
+                            scale=inv_r[:, b - first, h : h + 1],
+                        )
+            elif step == 5:
+                for b in images:
+                    tokT = proj_psum.tile([P, H, PACK, P], BF16, name="proj")
+                    for h in range(H):
+                        for t in range(PACK):
+                            nc.tensor.transpose(
+                                tokT[:, h, t, :],
+                                closing[b, "tokens"][:, h, t * P : (t + 1) * P],
+                                ident_bf[:],
+                            )
+                    grouped = tail_pool.tile([P, H, P, PACK], BF16, name="grouped", align_bytes=64)
+                    closing[b, "grouped"] = grouped
+                    nc.scalar.copy(out=grouped[:], in_=tokT[:].rearrange("p h t r -> p h r t"))
             else:
-                project(first + step - 2)
+                for b in images:
+                    codes = tail_pool.tile([P, H * P], U32, name="codes", align_bytes=64)
+                    scales = tail_pool.tile([P, H * P], U8, name="scales", align_bytes=64)
+                    nc.vector.quantize_mx(
+                        out=codes[:].bitcast(FP8X4),
+                        scales=scales[:],
+                        in_=closing[b, "grouped"][:].rearrange("p h r t -> p (h r t)"),
+                    )
+                    closing[b, "codes"] = codes
+                    closing[b, "scales"] = scales
+                for b in images:
+                    product = proj_psum.tile([P, H, F], F32, name="proj")
+                    for h in range(H):
+                        nc.tensor.matmul_mx(
+                            out=product[:, h, :],
+                            lhsT=closing[b, "codes"][:, h * P : (h + 1) * P].bitcast(FP8X4),
+                            lhsT_scale=closing[b, "scales"][:, h * P : (h + 1) * P],
+                            rhs=w_codes[:].bitcast(FP8X4),
+                            rhs_scale=w_scales[:],
+                            start=True,
+                            stop=True,
+                        )
+                    nc.vector.tensor_tensor(
+                        out=pre_act[:, b],
+                        in0=product[:],
+                        in1=bias[:].unsqueeze(1).to_broadcast([P, H, F]),
+                        op=ALU.add,
+                    )
 
-        transpose_x(0)
-        cube_x(0)
-        for k in range(K):
-            square_products(0, k)
-        coefficients(0)
-        transpose_p(0, 0)
-        transpose_x(1)
-        cube_x(1)
+        for b in range(2):
+            prepare(b)
+            for k in range(1, K):
+                sum_products(b, k)
+            start_coefficients(b)
+        finish_coefficients(0)
+        scale_cubes(0)
 
         for b in range(B):
-            for ch in range(CH):
-                if b + 1 < B:
-                    for k in range(ch * Z_PER_QUARTER, min(K, (ch + 1) * Z_PER_QUARTER)):
-                        square_products(b + 1, k)
-                window_terms(b, ch)
-                if ch + 1 < CH:
-                    transpose_p(b, ch + 1)
-                elif b + 1 < B:
-                    coefficients(b + 1)
-                    transpose_p(b + 1, 0)
-                    if b + 2 < B:
-                        transpose_x(b + 2)
-                        cube_x(b + 2)
-                window_sum(b, ch)
-                if b >= ROUND and b % ROUND == 0:
-                    close_round(b - ROUND, ch)
-            save_sum(b)
-        for step in range(CH):
-            close_round(B - ROUND, step)
+            if b + 2 < B:
+                prepare(b + 2)
+            for pair in range(CH // PAIR):
+                window_terms(b, pair)
+                window_sum(b, pair)
+            if b + 1 < B:
+                finish_coefficients(b + 1)
+                scale_cubes(b + 1)
+            if b + 2 < B:
+                first = (b - 1) // ROUND * ROUND
+                for k in range(1, K):
+                    sum_products(b + 2, k)
+                    slot = (b - first - 1) * (K - 1) + k - 1
+                    if first >= 0 and slot % 2 == 1:
+                        close_round(first)
+                start_coefficients(b + 2)
+        for first in range(0, B, ROUND):
+            while steps_done.get(first, 0) < CLOSING_STEPS:
+                close_round(first)
 
         stored = out.rearrange("b (h p) f -> p b h f", p=P)
         for first in range(0, B, ROUND):

@@ -28,6 +28,7 @@ K = len(OFFSETS)
 K_LEFT = OFFSETS.index((0, -1))
 TERMS = [(k, 0) for k in range(K)] + [(K_LEFT, 1)]
 
+MAX_TOP = 2
 PADDED = GRID + 2
 TERM_COLS = T + 4
 
@@ -36,7 +37,7 @@ EPS_NORM_SQUARED = 1e-24
 
 PAIR = 2
 ROUND = 2
-CLOSING_STEPS = 7
+CLOSING_STEPS = 8
 
 
 def tile_tokenmudule_pa_s_kernel(tc, patch_tokens, fc1_w, fc1_b, out):
@@ -79,13 +80,18 @@ def tile_tokenmudule_pa_s_kernel(tc, patch_tokens, fc1_w, fc1_b, out):
         minus_eps = keep.tile([P, 1], F32)
         nc.vector.memset(minus_eps[:], -EPS_GEM_CUBED)
 
-        q_pad = [keep.tile([P, CH, GRID, PADDED], F32, name="q_pad%d" % i) for i in range(2)]
-        p_pad = [keep.tile([P, CH, GRID, PADDED], F32, name="p_pad%d" % i) for i in range(2)]
+        q_pad = keep.tile([P, B, CH, GRID, PADDED], F32)
+        p_pad = keep.tile([P, 2, CH, GRID, PADDED], F32)
+        for padded in (q_pad, p_pad):
+            rows = padded[:].rearrange("p b c i j -> p (b c i) j")
+            nc.vector.memset(rows[:, :, 0:2], 0.0)
+            nc.vector.memset(rows[:, :, PADDED - 2 : PADDED], 0.0)
         term_tiles = [
             keep.tile([P, K, PAIR, TERM_COLS], F32, name="terms%d" % i) for i in range(3)
         ]
-        for zeroed in q_pad + p_pad + term_tiles:
-            nc.vector.memset(zeroed[:], 0.0)
+        for terms in term_tiles:
+            nc.vector.memset(terms[:, :, :, T - 1 : TERM_COLS], 0.0)
+            nc.vector.memset(terms[:, :, :, 0 : MAX_TOP * GRID], 0.0)
 
         w_grouped = keep.tile([P, F, PACK], BF16, align_bytes=64)
         w_codes = keep.tile([P, F], U32, align_bytes=64)
@@ -97,11 +103,11 @@ def tile_tokenmudule_pa_s_kernel(tc, patch_tokens, fc1_w, fc1_b, out):
             in_=w_grouped[:].rearrange("p f t -> p (f t)"),
         )
 
+        own_sq = keep.tile([P, B, CH], F32)
         pre_act = keep.tile([P, B, H, F], F32)
         result = keep.tile([P, B, H, F], F32)
 
         xT = {}
-        own_sq = {}
         norm_sq = {}
         norm = {}
         inv_norm = {}
@@ -117,7 +123,7 @@ def tile_tokenmudule_pa_s_kernel(tc, patch_tokens, fc1_w, fc1_b, out):
         def shifted(padded, top, dj):
             return padded[:, 0 : GRID - top, 1 + dj : 1 + dj + GRID]
 
-        def prepare(b):
+        def transpose_x(b):
             xT[b] = xT_psum.tile([P, CH, T], BF16, name="xT")
             for h in range(H):
                 for ch in range(CH):
@@ -126,20 +132,22 @@ def tile_tokenmudule_pa_s_kernel(tc, patch_tokens, fc1_w, fc1_b, out):
                         x_nat[:, b, h, ch * P : (ch + 1) * P],
                         ident_bf[:],
                     )
-            q = q_pad[b % 2]
+
+        def square_x(b):
+            transpose_x(b)
+            q = q_pad[:, b]
             nc.scalar.activation(
                 out=q[:, :, :, 1 : 1 + GRID],
                 in_=xT[b][:].rearrange("p c (i j) -> p c i j", j=GRID),
                 func=ACT.Square,
             )
-            own_sq[b] = coef_pool.tile([P, CH], F32, name="own_sq")
             for ch in range(CH):
                 unread = unread_pool.tile([P, GRID, PADDED], BF16, name="unread_s")
                 nc.scalar.activation(
                     out=unread[:],
                     in_=q[:, ch],
                     func=ACT.Square,
-                    accum_out=own_sq[b][:, ch : ch + 1],
+                    accum_out=own_sq[:, b, ch : ch + 1],
                 )
 
         def sum_products(b, k):
@@ -147,7 +155,7 @@ def tile_tokenmudule_pa_s_kernel(tc, patch_tokens, fc1_w, fc1_b, out):
                 norm_sq[b] = coef_pool.tile([P, K, CH], F32, name="norm_sq")
             di, dj = OFFSETS[k]
             top = -di
-            q = q_pad[b % 2]
+            q = q_pad[:, b]
             for ch in range(CH):
                 unread = unread_pool.tile([P, GRID, GRID], F32, name="unread_v")
                 nc.vector.scalar_tensor_tensor(
@@ -162,7 +170,7 @@ def tile_tokenmudule_pa_s_kernel(tc, patch_tokens, fc1_w, fc1_b, out):
 
         def start_coefficients(b):
             floored = coef_pool.tile([P, K, CH], F32, name="n_floored")
-            nc.vector.tensor_scalar_max(floored[:, 0, :], own_sq[b][:], EPS_NORM_SQUARED)
+            nc.vector.tensor_scalar_max(floored[:, 0, :], own_sq[:, b, :], EPS_NORM_SQUARED)
             nc.vector.tensor_scalar_max(floored[:, 1:K, :], norm_sq[b][:, 1:K, :], EPS_NORM_SQUARED)
             norm[b] = coef_pool.tile([P, K, CH], F32, name="norm")
             nc.scalar.activation(out=norm[b][:], in_=floored[:], func=ACT.Sqrt)
@@ -187,8 +195,8 @@ def tile_tokenmudule_pa_s_kernel(tc, patch_tokens, fc1_w, fc1_b, out):
         def scale_cubes(b):
             for ch in range(CH):
                 nc.vector.scalar_tensor_tensor(
-                    out=p_pad[b % 2][:, ch, :, 1 : 1 + GRID],
-                    in0=q_pad[b % 2][:, ch, :, 1 : 1 + GRID],
+                    out=p_pad[:, b % 2, ch, :, 1 : 1 + GRID],
+                    in0=q_pad[:, b, ch, :, 1 : 1 + GRID],
                     scalar=inv_norm[b][:, 0, ch : ch + 1],
                     in1=grid(xT[b][:, ch, :]),
                     op0=ALU.mult,
@@ -198,16 +206,22 @@ def tile_tokenmudule_pa_s_kernel(tc, patch_tokens, fc1_w, fc1_b, out):
         def window_terms(b, pair):
             terms = term_tiles[(b * (CH // PAIR) + pair) % 3]
             chunks = slice(pair * PAIR, (pair + 1) * PAIR)
-            p = p_pad[b % 2]
+            p = p_pad[:, b % 2]
             for k in range(K):
                 di, dj = OFFSETS[k]
                 top = -di
-                nc.vector.tensor_tensor(
-                    out=terms[:, k, :, top * GRID : T].rearrange("p c (i j) -> p c i j", j=GRID),
-                    in0=p[:, chunks, top:GRID, 1 : 1 + GRID],
-                    in1=p[:, chunks, 0 : GRID - top, 1 + dj : 1 + dj + GRID],
-                    op=ALU.mult,
-                )
+                products = terms[:, k, :, top * GRID : T].rearrange("p c (i j) -> p c i j", j=GRID)
+                if k == 0:
+                    nc.scalar.activation(
+                        out=products, in_=p[:, chunks, :, 1 : 1 + GRID], func=ACT.Square
+                    )
+                else:
+                    nc.vector.tensor_tensor(
+                        out=products,
+                        in0=p[:, chunks, top:GRID, 1 : 1 + GRID],
+                        in1=p[:, chunks, 0 : GRID - top, 1 + dj : 1 + dj + GRID],
+                        op=ALU.mult,
+                    )
                 for c in range(PAIR):
                     nc.scalar.activation(
                         out=terms[:, k, c, top * GRID : T],
@@ -235,7 +249,33 @@ def tile_tokenmudule_pa_s_kernel(tc, patch_tokens, fc1_w, fc1_b, out):
                             stop=(i == len(TERMS) - 1),
                         )
 
-        def close_round(first):
+        def square_sum(on_vector, values, unread, total):
+            if on_vector:
+                nc.vector.scalar_tensor_tensor(
+                    out=unread,
+                    in0=values,
+                    scalar=1.0,
+                    in1=values,
+                    op0=ALU.mult,
+                    op1=ALU.mult,
+                    accum_out=total,
+                )
+            else:
+                nc.scalar.activation(out=unread, in_=values, func=ACT.Square, accum_out=total)
+
+        def scale_rows(on_vector, scaled, values, factor):
+            if on_vector:
+                nc.vector.tensor_scalar_mul(scaled, values, factor)
+            else:
+                nc.scalar.activation(out=scaled, in_=values, func=ACT.Copy, scale=factor)
+
+        def copy_from_psum(on_vector, copied, values):
+            if on_vector:
+                nc.vector.tensor_copy(out=copied, in_=values)
+            else:
+                nc.scalar.copy(out=copied, in_=values)
+
+        def close_round(first, on_vector):
             step = steps_done.get(first, 0)
             steps_done[first] = step + 1
             images = range(first, first + ROUND)
@@ -256,53 +296,53 @@ def tile_tokenmudule_pa_s_kernel(tc, patch_tokens, fc1_w, fc1_b, out):
                         out=pooled[b][:], in_=pooled[b][:], func=ACT.Exp, scale=1.0 / 3.0
                     )
             elif step == 2:
-                r_sq = tail_pool.tile([P, ROUND, H], F32, name="r_sq")
-                closing[first, "r_sq"] = r_sq
                 for b in images:
                     nc.vector.tensor_tensor(
                         out=pooled[b][:], in0=pooled[b][:], in1=x_nat[:, b], op=ALU.add
                     )
-                    unread = tail_pool.tile([P, H, C], BF16, name="unread_r")
-                    for h in range(H):
-                        nc.scalar.activation(
-                            out=unread[:, h, :],
-                            in_=pooled[b][:, h, :],
-                            func=ACT.Square,
-                            accum_out=r_sq[:, b - first, h : h + 1],
-                        )
             elif step == 3:
+                r_sq = tail_pool.tile([P, ROUND, H], F32, name="r_sq")
+                closing[first, "r_sq"] = r_sq
+                for b in images:
+                    unread = tail_pool.tile([P, H, C], F32, name="unread_r")
+                    for h in range(H):
+                        square_sum(
+                            on_vector,
+                            pooled[b][:, h, :],
+                            unread[:, h, :],
+                            r_sq[:, b - first, h : h + 1],
+                        )
+            elif step == 4:
                 floored = tail_pool.tile([P, ROUND, H], F32, name="r_floored")
                 nc.vector.tensor_scalar_max(floored[:], closing[first, "r_sq"][:], EPS_NORM_SQUARED)
                 r_norm = tail_pool.tile([P, ROUND, H], F32, name="r_norm")
                 closing[first, "r_norm"] = r_norm
                 nc.scalar.activation(out=r_norm[:], in_=floored[:], func=ACT.Sqrt)
-            elif step == 4:
+            elif step == 5:
                 inv_r = tail_pool.tile([P, ROUND, H], F32, name="inv_r")
                 nc.vector.reciprocal(inv_r[:], closing[first, "r_norm"][:])
                 for b in images:
                     tokens = tail_pool.tile([P, H, C], BF16, name="tokens")
                     closing[b, "tokens"] = tokens
                     for h in range(H):
-                        nc.scalar.activation(
-                            out=tokens[:, h, :],
-                            in_=pooled[b][:, h, :],
-                            func=ACT.Copy,
-                            scale=inv_r[:, b - first, h : h + 1],
+                        scale_rows(
+                            on_vector,
+                            tokens[:, h, :],
+                            pooled[b][:, h, :],
+                            inv_r[:, b - first, h : h + 1],
                         )
-            elif step == 5:
                 for b in images:
+                    tokens = closing[b, "tokens"]
                     tokT = proj_psum.tile([P, H, PACK, P], BF16, name="proj")
                     for h in range(H):
                         for t in range(PACK):
                             nc.tensor.transpose(
-                                tokT[:, h, t, :],
-                                closing[b, "tokens"][:, h, t * P : (t + 1) * P],
-                                ident_bf[:],
+                                tokT[:, h, t, :], tokens[:, h, t * P : (t + 1) * P], ident_bf[:]
                             )
                     grouped = tail_pool.tile([P, H, P, PACK], BF16, name="grouped", align_bytes=64)
                     closing[b, "grouped"] = grouped
-                    nc.scalar.copy(out=grouped[:], in_=tokT[:].rearrange("p h t r -> p h r t"))
-            else:
+                    copy_from_psum(on_vector, grouped[:], tokT[:].rearrange("p h t r -> p h r t"))
+            elif step == 6:
                 for b in images:
                     codes = tail_pool.tile([P, H * P], U32, name="codes", align_bytes=64)
                     scales = tail_pool.tile([P, H * P], U8, name="scales", align_bytes=64)
@@ -311,38 +351,40 @@ def tile_tokenmudule_pa_s_kernel(tc, patch_tokens, fc1_w, fc1_b, out):
                         scales=scales[:],
                         in_=closing[b, "grouped"][:].rearrange("p h r t -> p (h r t)"),
                     )
-                    closing[b, "codes"] = codes
-                    closing[b, "scales"] = scales
-                for b in images:
                     product = proj_psum.tile([P, H, F], F32, name="proj")
+                    closing[b, "product"] = product
                     for h in range(H):
                         nc.tensor.matmul_mx(
                             out=product[:, h, :],
-                            lhsT=closing[b, "codes"][:, h * P : (h + 1) * P].bitcast(FP8X4),
-                            lhsT_scale=closing[b, "scales"][:, h * P : (h + 1) * P],
+                            lhsT=codes[:, h * P : (h + 1) * P].bitcast(FP8X4),
+                            lhsT_scale=scales[:, h * P : (h + 1) * P],
                             rhs=w_codes[:].bitcast(FP8X4),
                             rhs_scale=w_scales[:],
                             start=True,
                             stop=True,
                         )
+            else:
+                for b in images:
                     nc.vector.tensor_tensor(
                         out=pre_act[:, b],
-                        in0=product[:],
+                        in0=closing[b, "product"][:],
                         in1=bias[:].unsqueeze(1).to_broadcast([P, H, F]),
                         op=ALU.add,
                     )
 
         for b in range(2):
-            prepare(b)
+            for i in range(B // 2):
+                square_x(b * (B // 2) + i)
             for k in range(1, K):
                 sum_products(b, k)
             start_coefficients(b)
+        transpose_x(0)
         finish_coefficients(0)
         scale_cubes(0)
 
         for b in range(B):
-            if b + 2 < B:
-                prepare(b + 2)
+            if b + 1 < B:
+                transpose_x(b + 1)
             for pair in range(CH // PAIR):
                 window_terms(b, pair)
                 window_sum(b, pair)
@@ -350,16 +392,16 @@ def tile_tokenmudule_pa_s_kernel(tc, patch_tokens, fc1_w, fc1_b, out):
                 finish_coefficients(b + 1)
                 scale_cubes(b + 1)
             if b + 2 < B:
-                first = (b - 1) // ROUND * ROUND
                 for k in range(1, K):
                     sum_products(b + 2, k)
-                    slot = (b - first - 1) * (K - 1) + k - 1
-                    if first >= 0 and slot % 2 == 1:
-                        close_round(first)
+                    if k % 2 == 0:
+                        for first in range(0, b, ROUND):
+                            if steps_done.get(first, 0) < CLOSING_STEPS:
+                                close_round(first, False)
                 start_coefficients(b + 2)
         for first in range(0, B, ROUND):
             while steps_done.get(first, 0) < CLOSING_STEPS:
-                close_round(first)
+                close_round(first, True)
 
         stored = out.rearrange("b (h p) f -> p b h f", p=P)
         for first in range(0, B, ROUND):

@@ -38,6 +38,7 @@ EPS_NORM_SQUARED = 1e-24
 PAIR = 2
 ROUND = 2
 CLOSING_STEPS = 8
+COEFFICIENT_STEPS = 3
 
 
 def tile_tokenmudule_pa_s_kernel(tc, patch_tokens, fc1_w, fc1_b, out):
@@ -82,10 +83,7 @@ def tile_tokenmudule_pa_s_kernel(tc, patch_tokens, fc1_w, fc1_b, out):
 
         q_pad = keep.tile([P, B, CH, GRID, PADDED], F32)
         p_pad = keep.tile([P, 2, CH, GRID, PADDED], F32)
-        for padded in (q_pad, p_pad):
-            rows = padded[:].rearrange("p b c i j -> p (b c i) j")
-            nc.vector.memset(rows[:, :, 0:2], 0.0)
-            nc.vector.memset(rows[:, :, PADDED - 2 : PADDED], 0.0)
+        nc.vector.memset(p_pad[:], 0.0)
         term_tiles = [
             keep.tile([P, K, PAIR, TERM_COLS], F32, name="terms%d" % i) for i in range(3)
         ]
@@ -96,12 +94,6 @@ def tile_tokenmudule_pa_s_kernel(tc, patch_tokens, fc1_w, fc1_b, out):
         w_grouped = keep.tile([P, F, PACK], BF16, align_bytes=64)
         w_codes = keep.tile([P, F], U32, align_bytes=64)
         w_scales = keep.tile([P, F], U8, align_bytes=64)
-        nc.vector.tensor_copy(out=w_grouped[:], in_=w_raw[:].rearrange("p t f -> p f t"))
-        nc.vector.quantize_mx(
-            out=w_codes[:].bitcast(FP8X4),
-            scales=w_scales[:],
-            in_=w_grouped[:].rearrange("p f t -> p (f t)"),
-        )
 
         own_sq = keep.tile([P, B, CH], F32)
         pre_act = keep.tile([P, B, H, F], F32)
@@ -111,6 +103,7 @@ def tile_tokenmudule_pa_s_kernel(tc, patch_tokens, fc1_w, fc1_b, out):
         norm_sq = {}
         norm = {}
         inv_norm = {}
+        ratio = {}
         coef = {}
         acc = {}
         pooled = {}
@@ -122,6 +115,14 @@ def tile_tokenmudule_pa_s_kernel(tc, patch_tokens, fc1_w, fc1_b, out):
 
         def shifted(padded, top, dj):
             return padded[:, 0 : GRID - top, 1 + dj : 1 + dj + GRID]
+
+        def quantise_weights():
+            nc.vector.tensor_copy(out=w_grouped[:], in_=w_raw[:].rearrange("p t f -> p f t"))
+            nc.vector.quantize_mx(
+                out=w_codes[:].bitcast(FP8X4),
+                scales=w_scales[:],
+                in_=w_grouped[:].rearrange("p f t -> p (f t)"),
+            )
 
         def transpose_x(b):
             xT[b] = xT_psum.tile([P, CH, T], BF16, name="xT")
@@ -136,6 +137,7 @@ def tile_tokenmudule_pa_s_kernel(tc, patch_tokens, fc1_w, fc1_b, out):
         def square_x(b):
             transpose_x(b)
             q = q_pad[:, b]
+            nc.vector.memset(q, 0.0)
             nc.scalar.activation(
                 out=q[:, :, :, 1 : 1 + GRID],
                 in_=xT[b][:].rearrange("p c (i j) -> p c i j", j=GRID),
@@ -175,22 +177,28 @@ def tile_tokenmudule_pa_s_kernel(tc, patch_tokens, fc1_w, fc1_b, out):
             norm[b] = coef_pool.tile([P, K, CH], F32, name="norm")
             nc.scalar.activation(out=norm[b][:], in_=floored[:], func=ACT.Sqrt)
 
-        def finish_coefficients(b):
+        def invert_norms(b):
             inv_norm[b] = coef_pool.tile([P, K, CH], F32, name="inv_norm")
             nc.vector.reciprocal(inv_norm[b][:], norm[b][:])
-            ratio = coef_pool.tile([P, K, CH], F32, name="ratio")
-            nc.vector.tensor_tensor(
-                out=ratio[:],
-                in0=inv_norm[b][:],
-                in1=norm[b][:, 0:1, :].to_broadcast([P, K, CH]),
-                op=ALU.mult,
-            )
-            ratio_sq = coef_pool.tile([P, K, CH], F32, name="ratio_sq")
-            nc.vector.tensor_tensor(out=ratio_sq[:], in0=ratio[:], in1=ratio[:], op=ALU.mult)
-            coef[b] = coef_pool.tile([P, K, CH], F32, name="coef")
-            nc.vector.tensor_tensor(
-                out=coef[b][:], in0=ratio_sq[:], in1=inv_norm[b][:], op=ALU.mult
-            )
+
+        def coefficient_step(b, step):
+            if step == 0:
+                ratio[b] = coef_pool.tile([P, K, CH], F32, name="ratio")
+                nc.vector.tensor_tensor(
+                    out=ratio[b][:],
+                    in0=inv_norm[b][:],
+                    in1=norm[b][:, 0:1, :].to_broadcast([P, K, CH]),
+                    op=ALU.mult,
+                )
+            elif step == 1:
+                nc.vector.tensor_tensor(
+                    out=ratio[b][:], in0=ratio[b][:], in1=ratio[b][:], op=ALU.mult
+                )
+            else:
+                coef[b] = coef_pool.tile([P, K, CH], F32, name="coef")
+                nc.vector.tensor_tensor(
+                    out=coef[b][:], in0=ratio[b][:], in1=inv_norm[b][:], op=ALU.mult
+                )
 
         def scale_cubes(b):
             for ch in range(CH):
@@ -207,29 +215,35 @@ def tile_tokenmudule_pa_s_kernel(tc, patch_tokens, fc1_w, fc1_b, out):
             terms = term_tiles[(b * (CH // PAIR) + pair) % 3]
             chunks = slice(pair * PAIR, (pair + 1) * PAIR)
             p = p_pad[:, b % 2]
-            for k in range(K):
-                di, dj = OFFSETS[k]
-                top = -di
-                products = terms[:, k, :, top * GRID : T].rearrange("p c (i j) -> p c i j", j=GRID)
-                if k == 0:
-                    nc.scalar.activation(
-                        out=products, in_=p[:, chunks, :, 1 : 1 + GRID], func=ACT.Square
-                    )
-                else:
-                    nc.vector.tensor_tensor(
-                        out=products,
-                        in0=p[:, chunks, top:GRID, 1 : 1 + GRID],
-                        in1=p[:, chunks, 0 : GRID - top, 1 + dj : 1 + dj + GRID],
-                        op=ALU.mult,
-                    )
+
+            def products(k):
+                return terms[:, k, :, -OFFSETS[k][0] * GRID : T].rearrange(
+                    "p c (i j) -> p c i j", j=GRID
+                )
+
+            def scale_and_clamp(k):
+                written = slice(-OFFSETS[k][0] * GRID, T)
                 for c in range(PAIR):
                     nc.scalar.activation(
-                        out=terms[:, k, c, top * GRID : T],
-                        in_=terms[:, k, c, top * GRID : T],
+                        out=terms[:, k, c, written],
+                        in_=terms[:, k, c, written],
                         func=ACT.Relu,
                         scale=coef[b][:, k, pair * PAIR + c : pair * PAIR + c + 1],
                         bias=minus_eps[:],
                     )
+
+            nc.scalar.activation(out=products(0), in_=p[:, chunks, :, 1 : 1 + GRID], func=ACT.Square)
+            for k in range(1, K):
+                di, dj = OFFSETS[k]
+                top = -di
+                nc.vector.tensor_tensor(
+                    out=products(k),
+                    in0=p[:, chunks, top:GRID, 1 : 1 + GRID],
+                    in1=p[:, chunks, 0 : GRID - top, 1 + dj : 1 + dj + GRID],
+                    op=ALU.mult,
+                )
+                scale_and_clamp(k)
+            scale_and_clamp(0)
 
         def window_sum(b, pair):
             terms = term_tiles[(b * (CH // PAIR) + pair) % 3]
@@ -378,9 +392,12 @@ def tile_tokenmudule_pa_s_kernel(tc, patch_tokens, fc1_w, fc1_b, out):
             for k in range(1, K):
                 sum_products(b, k)
             start_coefficients(b)
+        quantise_weights()
         transpose_x(0)
-        finish_coefficients(0)
+        invert_norms(0)
         scale_cubes(0)
+        for step in range(COEFFICIENT_STEPS):
+            coefficient_step(0, step)
 
         for b in range(B):
             if b + 1 < B:
@@ -389,15 +406,18 @@ def tile_tokenmudule_pa_s_kernel(tc, patch_tokens, fc1_w, fc1_b, out):
                 window_terms(b, pair)
                 window_sum(b, pair)
             if b + 1 < B:
-                finish_coefficients(b + 1)
+                invert_norms(b + 1)
                 scale_cubes(b + 1)
-            if b + 2 < B:
-                for k in range(1, K):
+            for k in range(1, K):
+                if b + 2 < B:
                     sum_products(b + 2, k)
-                    if k % 2 == 0:
-                        for first in range(0, b, ROUND):
-                            if steps_done.get(first, 0) < CLOSING_STEPS:
-                                close_round(first, False)
+                if k % 2 == 1 and k // 2 < COEFFICIENT_STEPS and b + 1 < B:
+                    coefficient_step(b + 1, k // 2)
+                if k % 2 == 0 and b + 2 < B:
+                    for first in range(0, b, ROUND):
+                        if steps_done.get(first, 0) < CLOSING_STEPS:
+                            close_round(first, False)
+            if b + 2 < B:
                 start_coefficients(b + 2)
         for first in range(0, B, ROUND):
             while steps_done.get(first, 0) < CLOSING_STEPS:

@@ -74,8 +74,6 @@ def tile_tokenmudule_pa_s_kernel(tc, patch_tokens, fc1_w, fc1_b, out):
 
         ident_bf = keep.tile([P, P], BF16)
         make_identity(nc, ident_bf[:])
-        ident_f = keep.tile([P, P], F32)
-        make_identity(nc, ident_f[:])
         plus_eps = keep.tile([P, 1], F32)
         nc.vector.memset(plus_eps[:], EPS_GEM_CUBED)
         minus_eps = keep.tile([P, 1], F32)
@@ -83,13 +81,24 @@ def tile_tokenmudule_pa_s_kernel(tc, patch_tokens, fc1_w, fc1_b, out):
 
         q_pad = keep.tile([P, B, CH, GRID, PADDED], F32)
         p_pad = keep.tile([P, 2, CH, GRID, PADDED], F32)
-        nc.vector.memset(p_pad[:], 0.0)
         term_tiles = [
             keep.tile([P, K, PAIR, TERM_COLS], F32, name="terms%d" % i) for i in range(3)
         ]
+
+        def zero_outer_columns(grids):
+            rows = grids.rearrange("p c i j -> p (c i) j")
+            nc.gpsimd.memset(rows[:, :, 0:2], 0.0)
+            nc.gpsimd.memset(rows[:, :, PADDED - 2 : PADDED], 0.0)
+
+        for b in range(B):
+            zero_outer_columns(q_pad[:, b])
+        for i in range(2):
+            zero_outer_columns(p_pad[:, i])
         for terms in term_tiles:
-            nc.vector.memset(terms[:, :, :, T - 1 : TERM_COLS], 0.0)
-            nc.vector.memset(terms[:, :, :, 0 : MAX_TOP * GRID], 0.0)
+            nc.gpsimd.memset(terms[:, :, :, T - 1 : TERM_COLS], 0.0)
+            nc.gpsimd.memset(terms[:, :, :, 0 : MAX_TOP * GRID], 0.0)
+        ident_f = keep.tile([P, P], F32)
+        make_identity(nc, ident_f[:])
 
         w_grouped = keep.tile([P, F, PACK], BF16, align_bytes=64)
         w_codes = keep.tile([P, F], U32, align_bytes=64)
@@ -137,7 +146,6 @@ def tile_tokenmudule_pa_s_kernel(tc, patch_tokens, fc1_w, fc1_b, out):
         def square_x(b):
             transpose_x(b)
             q = q_pad[:, b]
-            nc.vector.memset(q, 0.0)
             nc.scalar.activation(
                 out=q[:, :, :, 1 : 1 + GRID],
                 in_=xT[b][:].rearrange("p c (i j) -> p c i j", j=GRID),

from contextlib import ExitStack

import concourse.mybir as mybir
from concourse.masks import make_identity

F32 = mybir.dt.float32
BF16 = mybir.dt.bfloat16
U32 = mybir.dt.uint32
U8 = mybir.dt.uint8
FP8X4 = mybir.dt.float8_e4m3fn_x4
ALU = mybir.AluOpType
ACT = mybir.ActivationFunctionType

P = 128
B = 8
GRID = 16
T = GRID * GRID
H = T // P
C = 512
CH = C // P
F = 128
PACK = 4

FLOPS = 2 * B * T * C * F

OFFSETS = [(0, 0), (0, -1), (-1, -1), (-1, 0), (-1, 1), (-2, -1), (-2, 0), (-2, 1)]
K = len(OFFSETS)
K_LEFT = OFFSETS.index((0, -1))
TERMS = [(k, 0) for k in range(K)] + [(K_LEFT, 1)]

MAX_TOP = 2
PADDED = GRID + 2
TERM_COLS = T + 4

EPS_GEM_CUBED = 1e-18
EPS_NORM_SQUARED = 1e-24

PAIR = 2
ROUND = 2
CLOSING_STEPS = 8
COEFFICIENT_STEPS = 3


def tile_tokenmudule_pa_s_kernel(tc, patch_tokens, fc1_w, fc1_b, out):
    nc = tc.nc

    with ExitStack() as ctx:
        ctx.enter_context(tc.manual_schedule())

        def sbuf(name, bufs):
            return ctx.enter_context(tc.tile_pool(name=name, bufs=bufs))

        def psum(name, bufs):
            return ctx.enter_context(tc.psum_pool(name=name, bufs=bufs))

        keep = sbuf("keep", 1)
        unread_pool = sbuf("unread", 4)
        coef_pool = sbuf("coef", 2)
        pooled_pool = sbuf("pooled", 2 * ROUND)
        tail_pool = sbuf("tail", ROUND)
        xT_psum = psum("xT_psum", 2)
        acc_psum = psum("acc_psum", ROUND * H)
        proj_psum = psum("proj_psum", 2)

        x_nat = keep.tile([P, B, H, C], BF16)
        for b in range(B):
            nc.sync.dma_start(
                out=x_nat[:, b], in_=patch_tokens[b].rearrange("(h p) c -> p h c", p=P)
            )
        w_raw = keep.tile([P, PACK, F], BF16)
        nc.scalar.dma_start(out=w_raw[:], in_=fc1_w.rearrange("(t p) f -> p t f", p=P))
        bias = keep.tile([P, F], BF16)
        nc.scalar.dma_start(out=bias[:], in_=fc1_b.partition_broadcast(P))

        ident_bf = keep.tile([P, P], BF16)
        make_identity(nc, ident_bf[:])
        plus_eps = keep.tile([P, 1], F32)
        nc.vector.memset(plus_eps[:], EPS_GEM_CUBED)
        minus_eps = keep.tile([P, 1], F32)
        nc.vector.memset(minus_eps[:], -EPS_GEM_CUBED)

        q_pad = keep.tile([P, B, CH, GRID, PADDED], F32)
        p_pad = keep.tile([P, 2, CH, GRID, PADDED], F32)
        term_tiles = [
            keep.tile([P, K, PAIR, TERM_COLS], F32, name="terms%d" % i) for i in range(3)
        ]

        def zero_outer_columns(grids):
            rows = grids.rearrange("p c i j -> p (c i) j")
            nc.gpsimd.memset(rows[:, :, 0:2], 0.0)
            nc.gpsimd.memset(rows[:, :, PADDED - 2 : PADDED], 0.0)

        for b in range(B):
            zero_outer_columns(q_pad[:, b])
        for i in range(2):
            zero_outer_columns(p_pad[:, i])
        for terms in term_tiles:
            nc.gpsimd.memset(terms[:, :, :, T - 1 : TERM_COLS], 0.0)
            nc.gpsimd.memset(terms[:, :, :, 0 : MAX_TOP * GRID], 0.0)
        ident_f = keep.tile([P, P], F32)
        make_identity(nc, ident_f[:])

        w_grouped = keep.tile([P, F, PACK], BF16, align_bytes=64)
        w_codes = keep.tile([P, F], U32, align_bytes=64)
        w_scales = keep.tile([P, F], U8, align_bytes=64)

        own_sq = keep.tile([P, B, CH], F32)
        pre_act = keep.tile([P, B, H, F], F32)
        result = keep.tile([P, B, H, F], F32)

        xT = {}
        norm_sq = {}
        norm = {}
        inv_norm = {}
        ratio = {}
        coef = {}
        acc = {}
        pooled = {}
        closing = {}
        steps_done = {}

        def grid(ap):
            return ap.rearrange("p (i j) -> p i j", j=GRID)

        def shifted(padded, top, dj):
            return padded[:, 0 : GRID - top, 1 + dj : 1 + dj + GRID]

        def quantise_weights():
            nc.vector.tensor_copy(out=w_grouped[:], in_=w_raw[:].rearrange("p t f -> p f t"))
            nc.vector.quantize_mx(
                out=w_codes[:].bitcast(FP8X4),
                scales=w_scales[:],
                in_=w_grouped[:].rearrange("p f t -> p (f t)"),
            )

        def transpose_x(b):
            xT[b] = xT_psum.tile([P, CH, T], BF16, name="xT")
            for h in range(H):
                for ch in range(CH):
                    nc.tensor.transpose(
                        xT[b][:, ch, h * P : (h + 1) * P],
                        x_nat[:, b, h, ch * P : (ch + 1) * P],
                        ident_bf[:],
                    )

        def square_x(b):
            transpose_x(b)
            q = q_pad[:, b]
            nc.scalar.activation(
                out=q[:, :, :, 1 : 1 + GRID],
                in_=xT[b][:].rearrange("p c (i j) -> p c i j", j=GRID),
                func=ACT.Square,
            )
            for ch in range(CH):
                unread = unread_pool.tile([P, GRID, PADDED], BF16, name="unread_s")
                nc.scalar.activation(
                    out=unread[:],
                    in_=q[:, ch],
                    func=ACT.Square,
                    accum_out=own_sq[:, b, ch : ch + 1],
                )

        def sum_products(b, k):
            if k == 1:
                norm_sq[b] = coef_pool.tile([P, K, CH], F32, name="norm_sq")
            di, dj = OFFSETS[k]
            top = -di
            q = q_pad[:, b]
            for ch in range(CH):
                unread = unread_pool.tile([P, GRID, GRID], F32, name="unread_v")
                nc.vector.scalar_tensor_tensor(
                    out=unread[:, top:GRID, :],
                    in0=q[:, ch, top:GRID, 1 : 1 + GRID],
                    scalar=1.0,
                    in1=shifted(q[:, ch], top, dj),
                    op0=ALU.mult,
                    op1=ALU.mult,
                    accum_out=norm_sq[b][:, k, ch : ch + 1],
                )

        def start_coefficients(b):
            floored = coef_pool.tile([P, K, CH], F32, name="n_floored")
            nc.vector.tensor_scalar_max(floored[:, 0, :], own_sq[:, b, :], EPS_NORM_SQUARED)
            nc.vector.tensor_scalar_max(floored[:, 1:K, :], norm_sq[b][:, 1:K, :], EPS_NORM_SQUARED)
            norm[b] = coef_pool.tile([P, K, CH], F32, name="norm")
            nc.scalar.activation(out=norm[b][:], in_=floored[:], func=ACT.Sqrt)

        def invert_norms(b):
            inv_norm[b] = coef_pool.tile([P, K, CH], F32, name="inv_norm")
            nc.vector.reciprocal(inv_norm[b][:], norm[b][:])

        def coefficient_step(b, step):
            if step == 0:
                ratio[b] = coef_pool.tile([P, K, CH], F32, name="ratio")
                nc.vector.tensor_tensor(
                    out=ratio[b][:],
                    in0=inv_norm[b][:],
                    in1=norm[b][:, 0:1, :].to_broadcast([P, K, CH]),
                    op=ALU.mult,
                )
            elif step == 1:
                nc.vector.tensor_tensor(
                    out=ratio[b][:], in0=ratio[b][:], in1=ratio[b][:], op=ALU.mult
                )
            else:
                coef[b] = coef_pool.tile([P, K, CH], F32, name="coef")
                nc.vector.tensor_tensor(
                    out=coef[b][:], in0=ratio[b][:], in1=inv_norm[b][:], op=ALU.mult
                )

        def scale_cubes(b):
            for ch in range(CH):
                nc.vector.scalar_tensor_tensor(
                    out=p_pad[:, b % 2, ch, :, 1 : 1 + GRID],
                    in0=q_pad[:, b, ch, :, 1 : 1 + GRID],
                    scalar=inv_norm[b][:, 0, ch : ch + 1],
                    in1=grid(xT[b][:, ch, :]),
                    op0=ALU.mult,
                    op1=ALU.mult,
                )

        def window_terms(b, pair):
            terms = term_tiles[(b * (CH // PAIR) + pair) % 3]
            chunks = slice(pair * PAIR, (pair + 1) * PAIR)
            p = p_pad[:, b % 2]

            def products(k):
                return terms[:, k, :, -OFFSETS[k][0] * GRID : T].rearrange(
                    "p c (i j) -> p c i j", j=GRID
                )

            def scale_and_clamp(k):
                written = slice(-OFFSETS[k][0] * GRID, T)
                for c in range(PAIR):
                    nc.scalar.activation(
                        out=terms[:, k, c, written],
                        in_=terms[:, k, c, written],
                        func=ACT.Relu,
                        scale=coef[b][:, k, pair * PAIR + c : pair * PAIR + c + 1],
                        bias=minus_eps[:],
                    )

            nc.scalar.activation(out=products(0), in_=p[:, chunks, :, 1 : 1 + GRID], func=ACT.Square)
            for k in range(1, K):
                di, dj = OFFSETS[k]
                top = -di
                nc.vector.tensor_tensor(
                    out=products(k),
                    in0=p[:, chunks, top:GRID, 1 : 1 + GRID],
                    in1=p[:, chunks, 0 : GRID - top, 1 + dj : 1 + dj + GRID],
                    op=ALU.mult,
                )
                scale_and_clamp(k)
            scale_and_clamp(0)

        def window_sum(b, pair):
            terms = term_tiles[(b * (CH // PAIR) + pair) % 3]
            if pair == 0:
                for h in range(H):
                    acc[b, h] = acc_psum.tile([P, C], F32, name="acc")
            for c in range(PAIR):
                ch = pair * PAIR + c
                for i, (k, ahead) in enumerate(TERMS):
                    for h in range(H):
                        nc.tensor.matmul(
                            acc[b, h][:, ch * P : (ch + 1) * P],
                            lhsT=terms[:, k, c, ahead + h * P : ahead + (h + 1) * P],
                            rhs=ident_f[:],
                            is_transpose=True,
                            start=(i == 0),
                            stop=(i == len(TERMS) - 1),
                        )

        def square_sum(on_vector, values, unread, total):
            if on_vector:
                nc.vector.scalar_tensor_tensor(
                    out=unread,
                    in0=values,
                    scalar=1.0,
                    in1=values,
                    op0=ALU.mult,
                    op1=ALU.mult,
                    accum_out=total,
                )
            else:
                nc.scalar.activation(out=unread, in_=values, func=ACT.Square, accum_out=total)

        def scale_rows(on_vector, scaled, values, factor):
            if on_vector:
                nc.vector.tensor_scalar_mul(scaled, values, factor)
            else:
                nc.scalar.activation(out=scaled, in_=values, func=ACT.Copy, scale=factor)

        def copy_from_psum(on_vector, copied, values):
            if on_vector:
                nc.vector.tensor_copy(out=copied, in_=values)
            else:
                nc.scalar.copy(out=copied, in_=values)

        def close_round(first, on_vector):
            step = steps_done.get(first, 0)
            steps_done[first] = step + 1
            images = range(first, first + ROUND)
            if step == 0:
                for b in images:
                    pooled[b] = pooled_pool.tile([P, H, C], F32, name="pooled")
                    for h in range(H):
                        nc.scalar.activation(
                            out=pooled[b][:, h, :],
                            in_=acc[b, h][:],
                            func=ACT.Ln,
                            scale=1.0 / len(TERMS),
                            bias=plus_eps[:],
                        )
            elif step == 1:
                for b in images:
                    nc.scalar.activation(
                        out=pooled[b][:], in_=pooled[b][:], func=ACT.Exp, scale=1.0 / 3.0
                    )
            elif step == 2:
                for b in images:
                    nc.vector.tensor_tensor(
                        out=pooled[b][:], in0=pooled[b][:], in1=x_nat[:, b], op=ALU.add
                    )
            elif step == 3:
                r_sq = tail_pool.tile([P, ROUND, H], F32, name="r_sq")
                closing[first, "r_sq"] = r_sq
                for b in images:
                    unread = tail_pool.tile([P, H, C], F32, name="unread_r")
                    for h in range(H):
                        square_sum(
                            on_vector,
                            pooled[b][:, h, :],
                            unread[:, h, :],
                            r_sq[:, b - first, h : h + 1],
                        )
            elif step == 4:
                floored = tail_pool.tile([P, ROUND, H], F32, name="r_floored")
                nc.vector.tensor_scalar_max(floored[:], closing[first, "r_sq"][:], EPS_NORM_SQUARED)
                r_norm = tail_pool.tile([P, ROUND, H], F32, name="r_norm")
                closing[first, "r_norm"] = r_norm
                nc.scalar.activation(out=r_norm[:], in_=floored[:], func=ACT.Sqrt)
            elif step == 5:
                inv_r = tail_pool.tile([P, ROUND, H], F32, name="inv_r")
                nc.vector.reciprocal(inv_r[:], closing[first, "r_norm"][:])
                for b in images:
                    tokens = tail_pool.tile([P, H, C], BF16, name="tokens")
                    closing[b, "tokens"] = tokens
                    for h in range(H):
                        scale_rows(
                            on_vector,
                            tokens[:, h, :],
                            pooled[b][:, h, :],
                            inv_r[:, b - first, h : h + 1],
                        )
                for b in images:
                    tokens = closing[b, "tokens"]
                    tokT = proj_psum.tile([P, H, PACK, P], BF16, name="proj")
                    for h in range(H):
                        for t in range(PACK):
                            nc.tensor.transpose(
                                tokT[:, h, t, :], tokens[:, h, t * P : (t + 1) * P], ident_bf[:]
                            )
                    grouped = tail_pool.tile([P, H, P, PACK], BF16, name="grouped", align_bytes=64)
                    closing[b, "grouped"] = grouped
                    copy_from_psum(on_vector, grouped[:], tokT[:].rearrange("p h t r -> p h r t"))
            elif step == 6:
                for b in images:
                    codes = tail_pool.tile([P, H * P], U32, name="codes", align_bytes=64)
                    scales = tail_pool.tile([P, H * P], U8, name="scales", align_bytes=64)
                    nc.vector.quantize_mx(
                        out=codes[:].bitcast(FP8X4),
                        scales=scales[:],
                        in_=closing[b, "grouped"][:].rearrange("p h r t -> p (h r t)"),
                    )
                    product = proj_psum.tile([P, H, F], F32, name="proj")
                    closing[b, "product"] = product
                    for h in range(H):
                        nc.tensor.matmul_mx(
                            out=product[:, h, :],
                            lhsT=codes[:, h * P : (h + 1) * P].bitcast(FP8X4),
                            lhsT_scale=scales[:, h * P : (h + 1) * P],
                            rhs=w_codes[:].bitcast(FP8X4),
                            rhs_scale=w_scales[:],
                            start=True,
                            stop=True,
                        )
            else:
                for b in images:
                    nc.vector.tensor_tensor(
                        out=pre_act[:, b],
                        in0=closing[b, "product"][:],
                        in1=bias[:].unsqueeze(1).to_broadcast([P, H, F]),
                        op=ALU.add,
                    )

        for b in range(2):
            for i in range(B // 2):
                square_x(b * (B // 2) + i)
            for k in range(1, K):
                sum_products(b, k)
            start_coefficients(b)
        quantise_weights()
        transpose_x(0)
        invert_norms(0)
        scale_cubes(0)
        for step in range(COEFFICIENT_STEPS):
            coefficient_step(0, step)

        for b in range(B):
            if b + 1 < B:
                transpose_x(b + 1)
            for pair in range(CH // PAIR):
                window_terms(b, pair)
                window_sum(b, pair)
            if b + 1 < B:
                invert_norms(b + 1)
                scale_cubes(b + 1)
            for k in range(1, K):
                if b + 2 < B:
                    sum_products(b + 2, k)
                if k % 2 == 1 and k // 2 < COEFFICIENT_STEPS and b + 1 < B:
                    coefficient_step(b + 1, k // 2)
                if k % 2 == 0 and b + 2 < B:
                    for first in range(0, b, ROUND):
                        if steps_done.get(first, 0) < CLOSING_STEPS:
                            close_round(first, False)
            if b + 2 < B:
                start_coefficients(b + 2)
        for first in range(0, B, ROUND):
            while steps_done.get(first, 0) < CLOSING_STEPS:
                close_round(first, True)

        stored = out.rearrange("b (h p) f -> p b h f", p=P)
        for first in range(0, B, ROUND):
            images = slice(first, first + ROUND)
            nc.scalar.activation(out=result[:, images], in_=pre_act[:, images], func=ACT.Gelu)
            nc.sync.dma_start(out=stored[:, images], in_=result[:, images])
